import numpy as np
import ml_dtypes


def mxq(x, axis, fmt="e4m3"):
    dtype, down = {"e4m3": (ml_dtypes.float8_e4m3fn, 7), "e5m2": (ml_dtypes.float8_e5m2, 14)}[fmt]
    v = np.moveaxis(np.asarray(x, np.float32).astype(ml_dtypes.bfloat16).astype(np.float64), axis, -1)
    blocks = v.reshape(v.shape[:-1] + (-1, 32))
    amax = np.abs(blocks).max(-1, keepdims=True)
    byte = np.maximum(np.where(amax > 0, np.frexp(amax)[1] - 1 + 127, 0) - down, 1)
    scale = np.exp2(byte - 127.0)
    codes = (blocks / scale).astype(np.float32).astype(dtype).astype(np.float64)
    return np.moveaxis((codes * scale).reshape(v.shape), -1, axis)


WIDE = False


def mx_kscale(k):
    if not WIDE:
        return np.ones(k)
    levels = np.array([10, -10, 5, -5, 0])
    a = np.random.permutation(np.resize(levels, k // 512 * 4)).reshape(k // 512, 4)
    idx = np.arange(k)
    return np.exp2(a[idx // 512, idx % 128 // 32])


BF16 = ml_dtypes.bfloat16


def bf(x):
    return np.asarray(x, np.float32).astype(BF16)


def f64(x):
    return np.asarray(x).astype(np.float64)


B, L, H = 32, 256, 512
N_BAND = 5
A = 1.2 / H ** 0.25


def setup_inputs():
    s, t = mx_kscale(H), mx_kscale(H)
    return {"q": bf(np.random.standard_normal((B, L, H)) * s),
            "k": bf(np.random.standard_normal((B, L, H)) * s),
            "Wq": bf(np.random.standard_normal((H, H)) * A / np.sqrt(H) / s[None, :] * t[:, None]),
            "bq": bf(np.random.standard_normal(H) * 0.5 * A * t),
            "Wk": bf(np.random.standard_normal((H, H)) * A / np.sqrt(H) / s[None, :] / t[:, None]),
            "bk": bf(np.random.standard_normal(H) * 0.5 * A / t)}


def reference(q, k, Wq, bq, Wk, bk):
    b, l, e = q.shape
    qs = (mxq(f64(q), 2, "e4m3") @ mxq(f64(Wq), 1, "e4m3").T) + f64(bq)
    ks = (mxq(f64(k), 2, "e4m3") @ mxq(f64(Wk), 1, "e4m3").T) + f64(bk)
    logits = mxq(qs, 2, "e4m3") @ mxq(ks, 2, "e4m3").transpose(0, 2, 1)
    idx = np.arange(l)
    band = np.abs(idx[:, None] - idx[None, :]) <= (N_BAND - 1)
    logits = np.where(band[None, :, :], logits, -np.inf)
    z = np.exp(logits - logits.max(-1, keepdims=True))
    return z / z.sum(-1, keepdims=True)

@@ -1,0 +1,313 @@
+from contextlib import ExitStack
+
+import concourse.mybir as mybir
+from concourse.masks import make_identity
+
+F32 = mybir.dt.float32
+BF16 = mybir.dt.bfloat16
+U32 = mybir.dt.uint32
+U8 = mybir.dt.uint8
+FP8X4 = mybir.dt.float8_e4m3fn_x4
+ALU = mybir.AluOpType
+ACT = mybir.ActivationFunctionType
+
+P = 128
+B, L, H = 32, 256, 512
+BLK = 512
+NB = B * L // BLK
+WIN = 136
+C0 = (0, L - WIN)
+NEG = -1.0e30
+RAW_BUFS = 4
+NOUT = 3
+B_SEG = {"q": (0, 512), "k": (0, 256)}
+A_CHUNKS = {"q": (), "k": (256, 384)}
+
+FLOPS = 2 * 2 * B * L * H * H + 2 * B * L * L * H
+
+
+def tile_scoperecognizer_t_kernel(tc, q, k, Wq, bq, Wk, bk, out):
+    nc = tc.nc
+    src = {"q": q, "k": k}
+    wsrc = {"q": Wq, "k": Wk}
+    bsrc = {"q": bq, "k": bk}
+    T = {}
+    with ExitStack() as ctx:
+        const = ctx.enter_context(tc.tile_pool(name="const", bufs=1))
+        rawp = ctx.enter_context(tc.tile_pool(name="rawp", bufs=RAW_BUFS))
+        work = ctx.enter_context(tc.tile_pool(name="work", bufs=2))
+        pt = ctx.enter_context(tc.psum_pool(name="pt", bufs=2))
+        p1 = ctx.enter_context(tc.psum_pool(name="p1", bufs=4))
+        p2 = ctx.enter_context(tc.psum_pool(name="p2", bufs=2))
+        ctx.enter_context(tc.manual_schedule())
+
+        def ok(i):
+            return 0 <= i < NB
+
+        def load(t, i):
+            if not ok(i):
+                return
+            r = rawp.tile([P, 4 * BLK], BF16, name="raw_" + t, tag="raw_" + t)
+            nc.sync.dma_start(
+                out=r[:].rearrange("p (b x) -> p b x", b=2),
+                in_=src[t][2 * i : 2 * i + 2].rearrange("b (p s) c -> p b (s c)", s=2),
+            )
+            T[("raw", t, i)] = r
+
+        wraw = {}
+        braw = {}
+        for t in ("q", "k"):
+            braw[t] = const.tile([P, 4], BF16, name="braw_" + t)
+            nc.scalar.dma_start(out=braw[t][:], in_=bsrc[t].rearrange("(m j) -> m j", j=4))
+        for t in ("q", "k"):
+            wraw[t] = const.tile([P, 4 * H], BF16, name="wraw_" + t)
+            nc.sync.dma_start(out=wraw[t][:], in_=wsrc[t].rearrange("(m j) c -> m (j c)", j=4))
+            load(t, 0)
+        for i in range(1, RAW_BUFS):
+            load("q", i)
+            load("k", i)
+
+        ident = const.tile([P, P], F32, name="ident")
+        make_identity(nc, ident[:])
+        warm = const.tile([P, 1], F32, name="warm")
+        warm2 = const.tile([P, 1], F32, name="warm2")
+        nc.vector.memset(warm[:], 0.0)
+        nc.scalar.activation(out=warm2[:], in_=warm[:], func=ACT.Exp)
+        mask = const.tile([P, 2, WIN], F32, name="mask")
+        nc.gpsimd.memset(mask[:], 0.0)
+        for h in range(2):
+            d = h * P - C0[h]
+            nc.gpsimd.affine_select(
+                out=mask[:, 1 - h, :], in_=mask[:, 1 - h, :], compare_op=ALU.is_ge, fill=NEG,
+                base=4 - d, pattern=[[1, WIN]], channel_multiplier=-1,
+            )
+            nc.gpsimd.affine_select(
+                out=mask[:, 1 - h, :], in_=mask[:, 1 - h, :], compare_op=ALU.is_ge, fill=NEG,
+                base=4 + d, pattern=[[-1, WIN]], channel_multiplier=1,
+            )
+        outs = []
+        for n in range(NOUT):
+            o = const.tile([P, 4, L], F32, name="o%d" % n)
+            nc.gpsimd.memset(o[:], 0.0)
+            outs.append(o)
+        bias = {}
+        for t in ("q", "k"):
+            bias[t] = const.tile([P, 4], F32, name="bias_" + t)
+            nc.vector.tensor_copy(out=bias[t][:], in_=braw[t][:])
+
+        W = {}
+        gw = {}
+        for t in ("q", "k"):
+            wf = wraw[t][:].bitcast(F32)
+            gw[t] = const.tile([P, 4 * H], BF16, name="gw_" + t, align_bytes=64)
+            gf = gw[t][:].bitcast(F32)
+            for jj in range(2):
+                if t == "q":
+                    ps = pt.tile([P, 4, P], F32, name="pTw", tag="pT")
+                else:
+                    ps = p1.tile([P, 4, P], F32, name="p1w", tag="p1")
+                for g in range(4):
+                    c = (4 * jj + g) * P
+                    nc.tensor.transpose(out=ps[:, g, :], in_=wf[:, c : c + P], identity=ident[:])
+                dst = gf[:, jj * 512 : (jj + 1) * 512].rearrange("p (a m u) -> p a m u", a=2, u=2)
+                s_ = ps[:].rearrange("p (a u) m -> p a m u", a=2)
+                if jj == 0:
+                    nc.scalar.copy(out=dst, in_=s_)
+                else:
+                    nc.vector.tensor_copy(out=dst, in_=s_)
+        for t in ("q", "k"):
+            cw = const.tile([P, H], U32, name="cw_" + t, align_bytes=64)
+            sw = const.tile([P, H], U8, name="sw_" + t, align_bytes=64)
+            nc.vector.quantize_mx(out=cw[:].bitcast(FP8X4), scales=sw[:], in_=gw[t][:])
+            W[t] = (cw, sw)
+
+        def transposes(t, i):
+            if not ok(i):
+                return
+            rf = T[("raw", t, i)][:].bitcast(F32)
+            for bb in range(2):
+                ps = pt.tile([P, 4, P], F32, name="pT", tag="pT")
+                for g in range(4):
+                    c = (4 * bb + g) * P
+                    nc.tensor.transpose(out=ps[:, g, :], in_=rf[:, c : c + P], identity=ident[:])
+                T[("pT", t, i, bb)] = ps
+            load(t, i + RAW_BUFS)
+
+        def tev(t, i):
+            if not ok(i):
+                return
+            g_ = work.tile([P, 4 * BLK], BF16, name="gin_" + t, tag="gin_" + t, align_bytes=64)
+            gf = g_[:].bitcast(F32)
+            for bb in range(2):
+                nc.scalar.copy(
+                    out=gf[:, bb * 512 : (bb + 1) * 512].rearrange("p (r g) -> p r g", g=4),
+                    in_=T[("pT", t, i, bb)][:].rearrange("p g r -> p r g"),
+                )
+            T[("gin", t, i)] = g_
+
+        def quantise(kind, t, i):
+            if not ok(i):
+                return
+            cod = work.tile([P, BLK], U32, name="c" + kind + t, tag="c" + kind + t, align_bytes=64)
+            sca = work.tile([P, BLK], U8, name="s" + kind + t, tag="s" + kind + t, align_bytes=64)
+            nc.vector.quantize_mx(out=cod[:].bitcast(FP8X4), scales=sca[:], in_=T[("g" + kind, t, i)][:])
+            T[("c" + kind, t, i)] = (cod, sca)
+
+        def mx(o, lc, ls, l0, rc, rs, r0, n):
+            nc.tensor.matmul_mx(
+                out=o,
+                lhsT=lc[:, l0 : l0 + P].bitcast(FP8X4), lhsT_scale=ls[:, l0 : l0 + P],
+                rhs=rc[:, r0 : r0 + n].bitcast(FP8X4), rhs_scale=rs[:, r0 : r0 + n],
+                start=True, stop=True,
+            )
+
+        def m1b(t, i):
+            if not ok(i):
+                return
+            tok0, n = B_SEG[t]
+            per = 512 // n
+            cod, sca = T[("cin", t, i)]
+            ps = None
+            for j in range(4):
+                if j % per == 0:
+                    ps = p1.tile([P, 512], F32, name="p1b", tag="p1")
+                o = ps[:, (j % per) * n : (j % per + 1) * n]
+                mx(o, W[t][0], W[t][1], j * P, cod, sca, tok0, n)
+                T[("p1b", t, i, j)] = o
+
+        def m1a(t, i):
+            if not ok(i):
+                return
+            cod, sca = T[("cin", t, i)]
+            for c in A_CHUNKS[t]:
+                ps = p1.tile([P, 4, P], F32, name="p1a", tag="p1")
+                for j in range(4):
+                    mx(ps[:, j, :], W[t][0], W[t][1], j * P, cod, sca, c, P)
+                T[("p1a", t, i, c)] = ps
+
+        def s1(t, i):
+            if not ok(i):
+                return
+            n = B_SEG[t][1]
+            st = work.tile([P, 4, n], BF16, name="st_" + t, tag="st_" + t)
+            for j in range(4):
+                nc.scalar.activation(
+                    out=st[:, j, :], in_=T[("p1b", t, i, j)], func=ACT.Identity,
+                    bias=bias[t][:, j : j + 1], scale=1.0,
+                )
+            T[("st", t, i)] = st
+
+        def gout(t, i):
+            if ("gout", t, i) not in T:
+                T[("gout", t, i)] = work.tile(
+                    [P, 4 * BLK], BF16, name="gout_" + t, tag="gout_" + t, align_bytes=64
+                )
+            return T[("gout", t, i)]
+
+        def a_evac(t, i):
+            if not ok(i):
+                return
+            go = gout(t, i)
+            for c in A_CHUNKS[t]:
+                nc.vector.tensor_tensor(
+                    out=go[:, 4 * c : 4 * (c + P)].rearrange("p (r j) -> p r j", j=4),
+                    in0=T[("p1a", t, i, c)][:].rearrange("p j r -> p r j"),
+                    in1=bias[t][:].unsqueeze(1).to_broadcast([P, P, 4]),
+                    op=ALU.add,
+                )
+
+        def regroup(t, i):
+            if not ok(i):
+                return
+            go = gout(t, i)
+            tok0, n = B_SEG[t]
+            nc.vector.tensor_copy(
+                out=go[:, 4 * tok0 : 4 * (tok0 + n)].rearrange("p (c i t) -> p c t i", i=4, t=4),
+                in_=T[("st", t, i)][:].rearrange("p t (c i) -> p c t i", i=4),
+            )
+
+        def m2(i):
+            if not ok(i):
+                return
+            qc, qs_ = T[("cout", "q", i)]
+            kc, ks_ = T[("cout", "k", i)]
+            for bb in range(2):
+                ps = p2.tile([P, 2, L], F32, name="p2t", tag="p2")
+                for h in range(2):
+                    mx(ps[:, 1 - h, :], qc, qs_, bb * L + h * P, kc, ks_, bb * L, L)
+                T[("p2", i, bb)] = ps
+
+        def ttr(i):
+            if not ok(i):
+                return
+            y = work.tile([P, 4, WIN], F32, name="y", tag="y")
+            nm = work.tile([P, 4], F32, name="nm", tag="nm")
+            for bb in range(2):
+                flat = T[("p2", i, bb)][:].rearrange("p a c -> p (a c)")
+                nc.vector.tensor_tensor(
+                    out=y[:, 2 * bb : 2 * bb + 2, :].rearrange("p a c -> p (a c)"),
+                    in0=flat[:, C0[1] : C0[1] + 2 * WIN],
+                    in1=mask[:].rearrange("p a c -> p (a c)"),
+                    op=ALU.add,
+                )
+            nc.vector.tensor_reduce(out=nm[:], in_=y[:], axis=mybir.AxisListType.X, op=ALU.max, negate=True)
+            T[("y", i)] = (y, nm)
+
+        def ex(i):
+            if not ok(i):
+                return
+            y, nm = T[("y", i)]
+            o = outs[i % NOUT]
+            sm = work.tile([P, 4], F32, name="sm", tag="sm")
+            for n in range(4):
+                h = 1 - n % 2
+                c = C0[h]
+                nc.scalar.activation(
+                    out=o[:, n - n % 2 + h, c : c + WIN], in_=y[:, n, :], func=ACT.Exp,
+                    bias=nm[:, n : n + 1], scale=1.0, accum_out=sm[:, n : n + 1],
+                )
+            T[("sm", i)] = sm
+
+        def recip(i):
+            if not ok(i):
+                return
+            rc = work.tile([P, 4], F32, name="rc", tag="rc")
+            nc.vector.reciprocal(out=rc[:], in_=T[("sm", i)][:])
+            T[("rc", i)] = rc
+
+        def norm(i):
+            if not ok(i):
+                return
+            o = outs[i % NOUT]
+            rc = T[("rc", i)]
+            for n in range(4):
+                h = 1 - n % 2
+                w = o[:, n - n % 2 + h, C0[h] : C0[h] + WIN]
+                nc.vector.tensor_scalar_mul(out=w, in0=w, scalar1=rc[:, n : n + 1])
+            nc.sync.dma_start(
+                out=out[2 * i : 2 * i + 2].rearrange("b (h p) j -> p (b h) j", p=P), in_=o[:]
+            )
+
+        transposes("q", 0)
+        for c in range(-1, NB + 3):
+            tev("q", c + 1)
+            regroup("k", c - 1)
+            recip(c - 3)
+            ttr(c - 2)
+            norm(c - 3)
+            transposes("k", c + 1)
+            s1("q", c)
+            quantise("out", "k", c - 1)
+            quantise("in", "q", c + 1)
+            m1a("k", c)
+            m1b("k", c)
+            a_evac("k", c)
+            tev("k", c + 1)
+            m2(c - 1)
+            regroup("q", c)
+            s1("k", c)
+            quantise("in", "k", c + 1)
+            transposes("q", c + 2)
+            quantise("out", "q", c)
+            m1b("q", c + 1)
+            ex(c - 2)

@@ -20,8 +20,7 @@ C0 = (0, L - WIN)
 NEG = -1.0e30
 RAW_BUFS = 4
 NOUT = 3
-B_SEG = {"q": (0, 512), "k": (0, 256)}
-A_CHUNKS = {"q": (), "k": (256, 384)}
+G_PIECES = 2
 
 FLOPS = 2 * 2 * B * L * H * H + 2 * B * L * L * H
 
@@ -60,9 +59,9 @@ def tile_scoperecognizer_t_kernel(tc, q, k, Wq, bq, Wk, bk, out):
             braw[t] = const.tile([P, 4], BF16, name="braw_" + t)
             nc.scalar.dma_start(out=braw[t][:], in_=bsrc[t].rearrange("(m j) -> m j", j=4))
         for t in ("q", "k"):
+            load(t, 0)
             wraw[t] = const.tile([P, 4 * H], BF16, name="wraw_" + t)
             nc.sync.dma_start(out=wraw[t][:], in_=wsrc[t].rearrange("(m j) c -> m (j c)", j=4))
-            load(t, 0)
         for i in range(1, RAW_BUFS):
             load("q", i)
             load("k", i)
@@ -95,30 +94,38 @@ def tile_scoperecognizer_t_kernel(tc, q, k, Wq, bq, Wk, bk, out):
             bias[t] = const.tile([P, 4], F32, name="bias_" + t)
             nc.vector.tensor_copy(out=bias[t][:], in_=braw[t][:])
 
+        def copy_out(eng, dst, s_):
+            if eng == "S":
+                nc.scalar.copy(out=dst, in_=s_)
+            else:
+                nc.vector.tensor_copy(out=dst, in_=s_)
+
         W = {}
-        gw = {}
-        for t in ("q", "k"):
+
+        def w_transposes(t):
             wf = wraw[t][:].bitcast(F32)
-            gw[t] = const.tile([P, 4 * H], BF16, name="gw_" + t, align_bytes=64)
-            gf = gw[t][:].bitcast(F32)
             for jj in range(2):
-                if t == "q":
-                    ps = pt.tile([P, 4, P], F32, name="pTw", tag="pT")
-                else:
-                    ps = p1.tile([P, 4, P], F32, name="p1w", tag="p1")
+                ps = p1.tile([P, 4, P], F32, name="p1w", tag="p1")
                 for g in range(4):
                     c = (4 * jj + g) * P
                     nc.tensor.transpose(out=ps[:, g, :], in_=wf[:, c : c + P], identity=ident[:])
-                dst = gf[:, jj * 512 : (jj + 1) * 512].rearrange("p (a m u) -> p a m u", a=2, u=2)
-                s_ = ps[:].rearrange("p (a u) m -> p a m u", a=2)
-                if jj == 0:
-                    nc.scalar.copy(out=dst, in_=s_)
-                else:
-                    nc.vector.tensor_copy(out=dst, in_=s_)
-        for t in ("q", "k"):
+                T[("pw", t, jj)] = ps
+
+        def w_evac(t, engs):
+            gw = const.tile([P, 4 * H], BF16, name="gw_" + t, align_bytes=64)
+            gf = gw[:].bitcast(F32)
+            for jj in range(2):
+                copy_out(
+                    engs[jj],
+                    gf[:, jj * 512 : (jj + 1) * 512].rearrange("p (a m u) -> p a m u", a=2, u=2),
+                    T[("pw", t, jj)][:].rearrange("p (a u) m -> p a m u", a=2),
+                )
+            T[("gw", t)] = gw
+
+        def w_quantise(t):
             cw = const.tile([P, H], U32, name="cw_" + t, align_bytes=64)
             sw = const.tile([P, H], U8, name="sw_" + t, align_bytes=64)
-            nc.vector.quantize_mx(out=cw[:].bitcast(FP8X4), scales=sw[:], in_=gw[t][:])
+            nc.vector.quantize_mx(out=cw[:].bitcast(FP8X4), scales=sw[:], in_=T[("gw", t)][:])
             W[t] = (cw, sw)
 
         def transposes(t, i):
@@ -133,15 +140,16 @@ def tile_scoperecognizer_t_kernel(tc, q, k, Wq, bq, Wk, bk, out):
                 T[("pT", t, i, bb)] = ps
             load(t, i + RAW_BUFS)
 
-        def tev(t, i):
+        def tev(t, i, engs):
             if not ok(i):
                 return
             g_ = work.tile([P, 4 * BLK], BF16, name="gin_" + t, tag="gin_" + t, align_bytes=64)
             gf = g_[:].bitcast(F32)
             for bb in range(2):
-                nc.scalar.copy(
-                    out=gf[:, bb * 512 : (bb + 1) * 512].rearrange("p (r g) -> p r g", g=4),
-                    in_=T[("pT", t, i, bb)][:].rearrange("p g r -> p r g"),
+                copy_out(
+                    engs[bb],
+                    gf[:, bb * 512 : (bb + 1) * 512].rearrange("p (r g) -> p r g", g=4),
+                    T[("pT", t, i, bb)][:].rearrange("p g r -> p r g"),
                 )
             T[("gin", t, i)] = g_
 
@@ -164,22 +172,17 @@ def tile_scoperecognizer_t_kernel(tc, q, k, Wq, bq, Wk, bk, out):
         def m1b(t, i):
             if not ok(i):
                 return
-            tok0, n = B_SEG[t]
-            per = 512 // n
             cod, sca = T[("cin", t, i)]
-            ps = None
             for j in range(4):
-                if j % per == 0:
-                    ps = p1.tile([P, 512], F32, name="p1b", tag="p1")
-                o = ps[:, (j % per) * n : (j % per + 1) * n]
-                mx(o, W[t][0], W[t][1], j * P, cod, sca, tok0, n)
-                T[("p1b", t, i, j)] = o
+                ps = p1.tile([P, BLK], F32, name="p1b", tag="p1")
+                mx(ps[:], W[t][0], W[t][1], j * P, cod, sca, 0, BLK)
+                T[("p1b", t, i, j)] = ps
 
         def m1a(t, i):
             if not ok(i):
                 return
             cod, sca = T[("cin", t, i)]
-            for c in A_CHUNKS[t]:
+            for c in range(0, BLK, P):
                 ps = p1.tile([P, 4, P], F32, name="p1a", tag="p1")
                 for j in range(4):
                     mx(ps[:, j, :], W[t][0], W[t][1], j * P, cod, sca, c, P)
@@ -188,11 +191,10 @@ def tile_scoperecognizer_t_kernel(tc, q, k, Wq, bq, Wk, bk, out):
         def s1(t, i):
             if not ok(i):
                 return
-            n = B_SEG[t][1]
-            st = work.tile([P, 4, n], BF16, name="st_" + t, tag="st_" + t)
+            st = work.tile([P, 4, BLK], BF16, name="st_" + t, tag="st_" + t)
             for j in range(4):
                 nc.scalar.activation(
-                    out=st[:, j, :], in_=T[("p1b", t, i, j)], func=ACT.Identity,
+                    out=st[:, j, :], in_=T[("p1b", t, i, j)][:], func=ACT.Identity,
                     bias=bias[t][:, j : j + 1], scale=1.0,
                 )
             T[("st", t, i)] = st
@@ -204,11 +206,11 @@ def tile_scoperecognizer_t_kernel(tc, q, k, Wq, bq, Wk, bk, out):
                 )
             return T[("gout", t, i)]
 
-        def a_evac(t, i):
+        def a_evac(t, i, chunks):
             if not ok(i):
                 return
             go = gout(t, i)
-            for c in A_CHUNKS[t]:
+            for c in chunks:
                 nc.vector.tensor_tensor(
                     out=go[:, 4 * c : 4 * (c + P)].rearrange("p (r j) -> p r j", j=4),
                     in0=T[("p1a", t, i, c)][:].rearrange("p j r -> p r j"),
@@ -220,11 +222,14 @@ def tile_scoperecognizer_t_kernel(tc, q, k, Wq, bq, Wk, bk, out):
             if not ok(i):
                 return
             go = gout(t, i)
-            tok0, n = B_SEG[t]
-            nc.vector.tensor_copy(
-                out=go[:, 4 * tok0 : 4 * (tok0 + n)].rearrange("p (c i t) -> p c t i", i=4, t=4),
-                in_=T[("st", t, i)][:].rearrange("p t (c i) -> p c t i", i=4),
-            )
+            st = T[("st", t, i)]
+            n = BLK // G_PIECES
+            for c in range(0, BLK, n):
+                nc.gpsimd.tensor_scalar(
+                    out=go[:, 4 * c : 4 * (c + n)].rearrange("p (r j) -> p r j", j=4),
+                    in0=st[:, :, c : c + n].rearrange("p j r -> p r j"),
+                    scalar1=1.0, scalar2=0.0, op0=ALU.mult, op1=ALU.add,
+                )
 
         def m2(i):
             if not ok(i):
@@ -237,11 +242,10 @@ def tile_scoperecognizer_t_kernel(tc, q, k, Wq, bq, Wk, bk, out):
                     mx(ps[:, 1 - h, :], qc, qs_, bb * L + h * P, kc, ks_, bb * L, L)
                 T[("p2", i, bb)] = ps
 
-        def ttr(i):
+        def madd(i):
             if not ok(i):
                 return
             y = work.tile([P, 4, WIN], F32, name="y", tag="y")
-            nm = work.tile([P, 4], F32, name="nm", tag="nm")
             for bb in range(2):
                 flat = T[("p2", i, bb)][:].rearrange("p a c -> p (a c)")
                 nc.vector.tensor_tensor(
@@ -250,20 +254,30 @@ def tile_scoperecognizer_t_kernel(tc, q, k, Wq, bq, Wk, bk, out):
                     in1=mask[:].rearrange("p a c -> p (a c)"),
                     op=ALU.add,
                 )
-            nc.vector.tensor_reduce(out=nm[:], in_=y[:], axis=mybir.AxisListType.X, op=ALU.max, negate=True)
-            T[("y", i)] = (y, nm)
+            T[("y", i)] = y
+
+        def rmax(i):
+            if not ok(i):
+                return
+            nm = work.tile([P, 4], F32, name="nm", tag="nm")
+            nc.vector.tensor_reduce(
+                out=nm[:], in_=T[("y", i)][:], axis=mybir.AxisListType.X, op=ALU.max, negate=True
+            )
+            T[("nm", i)] = nm
+
+        def window(i, n):
+            h = 1 - n % 2
+            return outs[i % NOUT][:, n - n % 2 + h, C0[h] : C0[h] + WIN]
 
         def ex(i):
             if not ok(i):
                 return
-            y, nm = T[("y", i)]
-            o = outs[i % NOUT]
+            y = T[("y", i)]
+            nm = T[("nm", i)]
             sm = work.tile([P, 4], F32, name="sm", tag="sm")
             for n in range(4):
-                h = 1 - n % 2
-                c = C0[h]
                 nc.scalar.activation(
-                    out=o[:, n - n % 2 + h, c : c + WIN], in_=y[:, n, :], func=ACT.Exp,
+                    out=window(i, n), in_=y[:, n, :], func=ACT.Exp,
                     bias=nm[:, n : n + 1], scale=1.0, accum_out=sm[:, n : n + 1],
                 )
             T[("sm", i)] = sm
@@ -275,39 +289,57 @@ def tile_scoperecognizer_t_kernel(tc, q, k, Wq, bq, Wk, bk, out):
             nc.vector.reciprocal(out=rc[:], in_=T[("sm", i)][:])
             T[("rc", i)] = rc
 
-        def norm(i):
+        def norm(i, tiles, eng):
             if not ok(i):
                 return
-            o = outs[i % NOUT]
             rc = T[("rc", i)]
-            for n in range(4):
-                h = 1 - n % 2
-                w = o[:, n - n % 2 + h, C0[h] : C0[h] + WIN]
-                nc.vector.tensor_scalar_mul(out=w, in0=w, scalar1=rc[:, n : n + 1])
+            for n in tiles:
+                w = window(i, n)
+                if eng == "V":
+                    nc.vector.tensor_scalar_mul(out=w, in0=w, scalar1=rc[:, n : n + 1])
+                else:
+                    nc.scalar.activation(out=w, in_=w, func=ACT.Copy, scale=rc[:, n : n + 1])
+
+        def store(i):
+            if not ok(i):
+                return
             nc.sync.dma_start(
-                out=out[2 * i : 2 * i + 2].rearrange("b (h p) j -> p (b h) j", p=P), in_=o[:]
+                out=out[2 * i : 2 * i + 2].rearrange("b (h p) j -> p (b h) j", p=P), in_=outs[i % NOUT][:]
             )
 
         transposes("q", 0)
+        w_transposes("q")
         for c in range(-1, NB + 3):
-            tev("q", c + 1)
-            regroup("k", c - 1)
-            recip(c - 3)
-            ttr(c - 2)
-            norm(c - 3)
+            first = c == -1
+            tev("q", c + 1, "SV" if first else "SS")
+            if first:
+                w_evac("q", "VS")
             transposes("k", c + 1)
+            if first:
+                w_transposes("k")
             s1("q", c)
+            recip(c - 2)
+            quantise("out", "q", c - 1)
             quantise("out", "k", c - 1)
-            quantise("in", "q", c + 1)
-            m1a("k", c)
-            m1b("k", c)
-            a_evac("k", c)
-            tev("k", c + 1)
             m2(c - 1)
+            quantise("in", "k", c)
+            if c == 0:
+                w_quantise("k")
+            m1a("k", c)
+            quantise("in", "q", c + 1)
+            if first:
+                w_quantise("q")
+            norm(c - 2, (0, 1), "V")
             regroup("q", c)
-            s1("k", c)
-            quantise("in", "k", c + 1)
+            madd(c - 1)
+            tev("k", c + 1, "SV" if first else "SS")
+            if first:
+                w_evac("k", "VS")
+            norm(c - 2, (2, 3), "S")
+            store(c - 2)
+            a_evac("k", c, (0,))
+            rmax(c - 1)
+            a_evac("k", c, (P, 2 * P, 3 * P))
             transposes("q", c + 2)
-            quantise("out", "q", c)
             m1b("q", c + 1)
-            ex(c - 2)
+            ex(c - 1)

@@ -5,6 +5,7 @@ from concourse.masks import make_identity
 
 F32 = mybir.dt.float32
 BF16 = mybir.dt.bfloat16
+I32 = mybir.dt.int32
 U32 = mybir.dt.uint32
 U8 = mybir.dt.uint8
 FP8X4 = mybir.dt.float8_e4m3fn_x4
@@ -15,12 +16,15 @@ P = 128
 B, L, H = 32, 256, 512
 BLK = 512
 NB = B * L // BLK
-WIN = 136
-C0 = (0, L - WIN)
+HALF = 64
+NS = L // HALF
+PADK = 8
+WIN = HALF + 2 * PADK
+KREG = 320
+QSLOT = 192
 NEG = -1.0e30
 RAW_BUFS = 4
 NOUT = 3
-G_PIECES = 2
 
 FLOPS = 2 * 2 * B * L * H * H + 2 * B * L * L * H
 
@@ -72,21 +76,54 @@ def tile_scoperecognizer_t_kernel(tc, q, k, Wq, bq, Wk, bk, out):
         warm2 = const.tile([P, 1], F32, name="warm2")
         nc.vector.memset(warm[:], 0.0)
         nc.scalar.activation(out=warm2[:], in_=warm[:], func=ACT.Exp)
-        mask = const.tile([P, 2, WIN], F32, name="mask")
-        nc.gpsimd.memset(mask[:], 0.0)
-        for h in range(2):
-            d = h * P - C0[h]
+
+        cq, sq, ck, sk, gk = [], [], [], [], []
+        for n in range(2):
+            cq.append(const.tile([P, NS * QSLOT], U32, name="cq%d" % n, align_bytes=64))
+            sq.append(const.tile([P, NS * QSLOT], U8, name="sq%d" % n, align_bytes=64))
+            ck.append(const.tile([P, 2 * KREG], U32, name="ck%d" % n, align_bytes=64))
+            sk.append(const.tile([P, 2 * KREG], U8, name="sk%d" % n, align_bytes=64))
+            gk.append(const.tile([P, 4 * 2 * KREG], BF16, name="gk%d" % n, align_bytes=64))
+            for x in (cq[n], sq[n], ck[n], sk[n]):
+                nc.vector.memset(x[:].bitcast(I32), 0)
+            for bb in range(2):
+                nc.vector.memset(gk[n][:, 4 * KREG * bb : 4 * (KREG * bb + PADK)], 0.0)
+                nc.vector.memset(gk[n][:, 4 * (KREG * bb + PADK + L) : 4 * (KREG * bb + L + 32)], 0.0)
+
+        m_lo = const.tile([P, WIN], F32, name="m_lo")
+        m_hi = const.tile([P, WIN], F32, name="m_hi")
+        for m_, off, side in ((m_lo, 0, -1), (m_hi, HALF, 1)):
+            nc.gpsimd.memset(m_[:], 0.0)
             nc.gpsimd.affine_select(
-                out=mask[:, 1 - h, :], in_=mask[:, 1 - h, :], compare_op=ALU.is_ge, fill=NEG,
-                base=4 - d, pattern=[[1, WIN]], channel_multiplier=-1,
+                out=m_[:], in_=m_[:], compare_op=ALU.is_ge, fill=NEG,
+                base=4 - PADK + off, pattern=[[1, WIN]], channel_multiplier=-1,
             )
             nc.gpsimd.affine_select(
-                out=mask[:, 1 - h, :], in_=mask[:, 1 - h, :], compare_op=ALU.is_ge, fill=NEG,
-                base=4 + d, pattern=[[-1, WIN]], channel_multiplier=1,
+                out=m_[:], in_=m_[:], compare_op=ALU.is_ge, fill=NEG,
+                base=4 + PADK - off, pattern=[[-1, WIN]], channel_multiplier=1,
             )
+            nc.gpsimd.affine_select(
+                out=m_[:], in_=m_[:], compare_op=ALU.is_ge, fill=NEG,
+                base=(HALF - 1) if side < 0 else -HALF, pattern=[[0, WIN]], channel_multiplier=side,
+            )
+        m_one = const.tile([P, WIN], F32, name="m_one")
+        mask = const.tile([P, NS, WIN], F32, name="mask")
+
+        def finish_mask():
+            nc.vector.tensor_tensor(out=m_one[:], in0=m_lo[:], in1=m_hi[:], op=ALU.max)
+            nc.vector.tensor_copy(out=mask[:], in_=m_one[:].unsqueeze(1).to_broadcast([P, NS, WIN]))
+            nc.gpsimd.affine_select(
+                out=mask[:, 0, :], in_=mask[:, 0, :], compare_op=ALU.is_ge, fill=NEG,
+                base=-PADK, pattern=[[1, WIN]], channel_multiplier=0,
+            )
+            nc.gpsimd.affine_select(
+                out=mask[:, NS - 1, :], in_=mask[:, NS - 1, :], compare_op=ALU.is_ge, fill=NEG,
+                base=WIN - PADK - 1, pattern=[[-1, WIN]], channel_multiplier=0,
+            )
+
         outs = []
         for n in range(NOUT):
-            o = const.tile([P, 4, L], F32, name="o%d" % n)
+            o = const.tile([P, NS, L], F32, name="o%d" % n)
             nc.gpsimd.memset(o[:], 0.0)
             outs.append(o)
         bias = {}
@@ -153,20 +190,20 @@ def tile_scoperecognizer_t_kernel(tc, q, k, Wq, bq, Wk, bk, out):
                 )
             T[("gin", t, i)] = g_
 
-        def quantise(kind, t, i):
+        def q1(t, i):
             if not ok(i):
                 return
-            cod = work.tile([P, BLK], U32, name="c" + kind + t, tag="c" + kind + t, align_bytes=64)
-            sca = work.tile([P, BLK], U8, name="s" + kind + t, tag="s" + kind + t, align_bytes=64)
-            nc.vector.quantize_mx(out=cod[:].bitcast(FP8X4), scales=sca[:], in_=T[("g" + kind, t, i)][:])
-            T[("c" + kind, t, i)] = (cod, sca)
+            cod = work.tile([P, BLK], U32, name="cin" + t, tag="cin" + t, align_bytes=64)
+            sca = work.tile([P, BLK], U8, name="sin" + t, tag="sin" + t, align_bytes=64)
+            nc.vector.quantize_mx(out=cod[:].bitcast(FP8X4), scales=sca[:], in_=T[("gin", t, i)][:])
+            T[("cin", t, i)] = (cod, sca)
 
-        def mx(o, lc, ls, l0, rc, rs, r0, n):
+        def mx(o, lc, ls, l0, rc, rs, r0, n, start, stop):
             nc.tensor.matmul_mx(
                 out=o,
                 lhsT=lc[:, l0 : l0 + P].bitcast(FP8X4), lhsT_scale=ls[:, l0 : l0 + P],
                 rhs=rc[:, r0 : r0 + n].bitcast(FP8X4), rhs_scale=rs[:, r0 : r0 + n],
-                start=True, stop=True,
+                start=start, stop=stop,
             )
 
         def m1b(t, i):
@@ -175,7 +212,7 @@ def tile_scoperecognizer_t_kernel(tc, q, k, Wq, bq, Wk, bk, out):
             cod, sca = T[("cin", t, i)]
             for j in range(4):
                 ps = p1.tile([P, BLK], F32, name="p1b", tag="p1")
-                mx(ps[:], W[t][0], W[t][1], j * P, cod, sca, 0, BLK)
+                mx(ps[:], W[t][0], W[t][1], j * P, cod, sca, 0, BLK, True, True)
                 T[("p1b", t, i, j)] = ps
 
         def m1a(t, i):
@@ -185,7 +222,7 @@ def tile_scoperecognizer_t_kernel(tc, q, k, Wq, bq, Wk, bk, out):
             for c in range(0, BLK, P):
                 ps = p1.tile([P, 4, P], F32, name="p1a", tag="p1")
                 for j in range(4):
-                    mx(ps[:, j, :], W[t][0], W[t][1], j * P, cod, sca, c, P)
+                    mx(ps[:, j, :], W[t][0], W[t][1], j * P, cod, sca, c, P, True, True)
                 T[("p1a", t, i, c)] = ps
 
         def s1(t, i):
@@ -199,93 +236,106 @@ def tile_scoperecognizer_t_kernel(tc, q, k, Wq, bq, Wk, bk, out):
                 )
             T[("st", t, i)] = st
 
-        def gout(t, i):
-            if ("gout", t, i) not in T:
-                T[("gout", t, i)] = work.tile(
-                    [P, 4 * BLK], BF16, name="gout_" + t, tag="gout_" + t, align_bytes=64
-                )
-            return T[("gout", t, i)]
-
-        def a_evac(t, i, chunks):
+        def a_evac(i, chunks):
             if not ok(i):
                 return
-            go = gout(t, i)
             for c in chunks:
+                c0 = 4 * (KREG * (c // L) + PADK + c % L)
                 nc.vector.tensor_tensor(
-                    out=go[:, 4 * c : 4 * (c + P)].rearrange("p (r j) -> p r j", j=4),
-                    in0=T[("p1a", t, i, c)][:].rearrange("p j r -> p r j"),
-                    in1=bias[t][:].unsqueeze(1).to_broadcast([P, P, 4]),
+                    out=gk[i % 2][:, c0 : c0 + 4 * P].rearrange("p (r j) -> p r j", j=4),
+                    in0=T[("p1a", "k", i, c)][:].rearrange("p j r -> p r j"),
+                    in1=bias["k"][:].unsqueeze(1).to_broadcast([P, P, 4]),
                     op=ALU.add,
                 )
 
-        def regroup(t, i):
+        def regroup(i):
             if not ok(i):
                 return
-            go = gout(t, i)
-            st = T[("st", t, i)]
-            n = BLK // G_PIECES
-            for c in range(0, BLK, n):
+            go = work.tile([P, 4 * BLK], BF16, name="gout_q", tag="gout_q", align_bytes=64)
+            st = T[("st", "q", i)]
+            dst = go[:].rearrange("p (s b r j) -> p b s r j", b=2, r=HALF, j=4)
+            for bb in range(2):
                 nc.gpsimd.tensor_scalar(
-                    out=go[:, 4 * c : 4 * (c + n)].rearrange("p (r j) -> p r j", j=4),
-                    in0=st[:, :, c : c + n].rearrange("p j r -> p r j"),
+                    out=dst[:, bb],
+                    in0=st[:, :, bb * L : (bb + 1) * L].rearrange("p j (s r) -> p s r j", r=HALF),
                     scalar1=1.0, scalar2=0.0, op0=ALU.mult, op1=ALU.add,
                 )
+            T[("gout", "q", i)] = go
+
+        def quant(gr, g0, cod, sca, c0, n):
+            nc.vector.quantize_mx(
+                out=cod[:, c0 : c0 + n].bitcast(FP8X4), scales=sca[:, c0 : c0 + n], in_=gr[:, 4 * g0 : 4 * (g0 + n)]
+            )
+
+        def q2q(i):
+            if not ok(i):
+                return
+            go = T[("gout", "q", i)]
+            quant(go, 0, cq[i % 2], sq[i % 2], 0, HALF)
+            for s in range(NS - 1):
+                quant(go, (2 * s + 1) * HALF, cq[i % 2], sq[i % 2], s * QSLOT + P, P)
+            quant(go, (2 * NS - 1) * HALF, cq[i % 2], sq[i % 2], (NS - 1) * QSLOT + P, HALF)
+
+        def q2k(i):
+            if not ok(i):
+                return
+            for bb in range(2):
+                quant(gk[i % 2], KREG * bb, ck[i % 2], sk[i % 2], KREG * bb, L)
+                quant(gk[i % 2], KREG * bb + L, ck[i % 2], sk[i % 2], KREG * bb + L, 32)
 
         def m2(i):
             if not ok(i):
                 return
-            qc, qs_ = T[("cout", "q", i)]
-            kc, ks_ = T[("cout", "k", i)]
-            for bb in range(2):
-                ps = p2.tile([P, 2, L], F32, name="p2t", tag="p2")
-                for h in range(2):
-                    mx(ps[:, 1 - h, :], qc, qs_, bb * L + h * P, kc, ks_, bb * L, L)
-                T[("p2", i, bb)] = ps
+            ps = p2.tile([P, NS, P], F32, name="p2t", tag="p2")
+            for s in range(NS):
+                for bb in range(2):
+                    mx(
+                        ps[:, s, :], cq[i % 2], sq[i % 2], s * QSLOT + bb * HALF,
+                        ck[i % 2], sk[i % 2], KREG * bb + s * HALF, P, bb == 0, bb == 1,
+                    )
+            T[("p2", i)] = ps
 
         def madd(i):
             if not ok(i):
                 return
-            y = work.tile([P, 4, WIN], F32, name="y", tag="y")
-            for bb in range(2):
-                flat = T[("p2", i, bb)][:].rearrange("p a c -> p (a c)")
-                nc.vector.tensor_tensor(
-                    out=y[:, 2 * bb : 2 * bb + 2, :].rearrange("p a c -> p (a c)"),
-                    in0=flat[:, C0[1] : C0[1] + 2 * WIN],
-                    in1=mask[:].rearrange("p a c -> p (a c)"),
-                    op=ALU.add,
-                )
+            y = work.tile([P, NS, WIN], F32, name="y", tag="y")
+            nc.vector.tensor_tensor(out=y[:], in0=T[("p2", i)][:, :, 0:WIN], in1=mask[:], op=ALU.add)
             T[("y", i)] = y
 
         def rmax(i):
             if not ok(i):
                 return
-            nm = work.tile([P, 4], F32, name="nm", tag="nm")
+            nm = work.tile([P, NS], F32, name="nm", tag="nm")
             nc.vector.tensor_reduce(
                 out=nm[:], in_=T[("y", i)][:], axis=mybir.AxisListType.X, op=ALU.max, negate=True
             )
             T[("nm", i)] = nm
 
-        def window(i, n):
-            h = 1 - n % 2
-            return outs[i % NOUT][:, n - n % 2 + h, C0[h] : C0[h] + WIN]
+        def span(s):
+            return (PADK if s == 0 else 0), (WIN - PADK if s == NS - 1 else WIN)
+
+        def window(i, s):
+            n0, n1 = span(s)
+            return outs[i % NOUT][:, s, s * HALF - PADK + n0 : s * HALF - PADK + n1]
 
         def ex(i):
             if not ok(i):
                 return
             y = T[("y", i)]
             nm = T[("nm", i)]
-            sm = work.tile([P, 4], F32, name="sm", tag="sm")
-            for n in range(4):
+            sm = work.tile([P, NS], F32, name="sm", tag="sm")
+            for s in range(NS):
+                n0, n1 = span(s)
                 nc.scalar.activation(
-                    out=window(i, n), in_=y[:, n, :], func=ACT.Exp,
-                    bias=nm[:, n : n + 1], scale=1.0, accum_out=sm[:, n : n + 1],
+                    out=window(i, s), in_=y[:, s, n0:n1], func=ACT.Exp,
+                    bias=nm[:, s : s + 1], scale=1.0, accum_out=sm[:, s : s + 1],
                 )
             T[("sm", i)] = sm
 
         def recip(i):
             if not ok(i):
                 return
-            rc = work.tile([P, 4], F32, name="rc", tag="rc")
+            rc = work.tile([P, NS], F32, name="rc", tag="rc")
             nc.vector.reciprocal(out=rc[:], in_=T[("sm", i)][:])
             T[("rc", i)] = rc
 
@@ -293,19 +343,21 @@ def tile_scoperecognizer_t_kernel(tc, q, k, Wq, bq, Wk, bk, out):
             if not ok(i):
                 return
             rc = T[("rc", i)]
-            for n in tiles:
-                w = window(i, n)
+            for s in tiles:
+                w = window(i, s)
                 if eng == "V":
-                    nc.vector.tensor_scalar_mul(out=w, in0=w, scalar1=rc[:, n : n + 1])
+                    nc.vector.tensor_scalar_mul(out=w, in0=w, scalar1=rc[:, s : s + 1])
                 else:
-                    nc.scalar.activation(out=w, in_=w, func=ACT.Copy, scale=rc[:, n : n + 1])
+                    nc.scalar.activation(out=w, in_=w, func=ACT.Copy, scale=rc[:, s : s + 1])
 
         def store(i):
             if not ok(i):
                 return
-            nc.sync.dma_start(
-                out=out[2 * i : 2 * i + 2].rearrange("b (h p) j -> p (b h) j", p=P), in_=outs[i % NOUT][:]
-            )
+            for bb in range(2):
+                nc.sync.dma_start(
+                    out=out[2 * i + bb].rearrange("(s p) j -> p s j", p=HALF),
+                    in_=outs[i % NOUT][bb * HALF : (bb + 1) * HALF, :, :],
+                )
 
         transposes("q", 0)
         w_transposes("q")
@@ -318,28 +370,30 @@ def tile_scoperecognizer_t_kernel(tc, q, k, Wq, bq, Wk, bk, out):
             if first:
                 w_transposes("k")
             s1("q", c)
-            recip(c - 2)
-            quantise("out", "q", c - 1)
-            quantise("out", "k", c - 1)
-            m2(c - 1)
-            quantise("in", "k", c)
+            recip(c - 3)
+            q1("k", c)
             if c == 0:
                 w_quantise("k")
             m1a("k", c)
-            quantise("in", "q", c + 1)
+            q2q(c - 1)
+            q2k(c - 1)
+            m2(c - 1)
+            q1("q", c + 1)
             if first:
                 w_quantise("q")
-            norm(c - 2, (0, 1), "V")
-            regroup("q", c)
-            madd(c - 1)
+            if c == 0:
+                finish_mask()
+            norm(c - 3, (0, 1), "V")
+            regroup(c)
+            madd(c - 2)
             tev("k", c + 1, "SV" if first else "SS")
             if first:
                 w_evac("k", "VS")
-            norm(c - 2, (2, 3), "S")
-            store(c - 2)
-            a_evac("k", c, (0,))
-            rmax(c - 1)
-            a_evac("k", c, (P, 2 * P, 3 * P))
+            norm(c - 3, (2, 3), "S")
+            store(c - 3)
+            a_evac(c, (0,))
+            rmax(c - 2)
+            a_evac(c, (P, 2 * P, 3 * P))
             transposes("q", c + 2)
             m1b("q", c + 1)
-            ex(c - 1)
+            ex(c - 2)

@@ -20,7 +20,8 @@ HALF = 64
 NS = L // HALF
 PADK = 8
 WIN = HALF + 2 * PADK
-KREG = 320
+GKW = 544
+CKW = 576
 QSLOT = 192
 NEG = -1.0e30
 RAW_BUFS = 4
@@ -81,14 +82,13 @@ def tile_scoperecognizer_t_kernel(tc, q, k, Wq, bq, Wk, bk, out):
         for n in range(2):
             cq.append(const.tile([P, NS * QSLOT], U32, name="cq%d" % n, align_bytes=64))
             sq.append(const.tile([P, NS * QSLOT], U8, name="sq%d" % n, align_bytes=64))
-            ck.append(const.tile([P, 2 * KREG], U32, name="ck%d" % n, align_bytes=64))
-            sk.append(const.tile([P, 2 * KREG], U8, name="sk%d" % n, align_bytes=64))
-            gk.append(const.tile([P, 4 * 2 * KREG], BF16, name="gk%d" % n, align_bytes=64))
+            ck.append(const.tile([P, CKW], U32, name="ck%d" % n, align_bytes=64))
+            sk.append(const.tile([P, CKW], U8, name="sk%d" % n, align_bytes=64))
+            gk.append(const.tile([P, 4 * GKW], BF16, name="gk%d" % n, align_bytes=64))
             for x in (cq[n], sq[n], ck[n], sk[n]):
                 nc.vector.memset(x[:].bitcast(I32), 0)
-            for bb in range(2):
-                nc.vector.memset(gk[n][:, 4 * KREG * bb : 4 * (KREG * bb + PADK)], 0.0)
-                nc.vector.memset(gk[n][:, 4 * (KREG * bb + PADK + L) : 4 * (KREG * bb + L + 32)], 0.0)
+            nc.vector.memset(gk[n][:, 0 : 4 * PADK], 0.0)
+            nc.vector.memset(gk[n][:, 4 * (PADK + BLK) : 4 * GKW], 0.0)
 
         m_lo = const.tile([P, WIN], F32, name="m_lo")
         m_hi = const.tile([P, WIN], F32, name="m_hi")
@@ -231,8 +231,9 @@ def tile_scoperecognizer_t_kernel(tc, q, k, Wq, bq, Wk, bk, out):
             st = work.tile([P, 4, BLK], BF16, name="st_" + t, tag="st_" + t)
             for j in range(4):
                 nc.scalar.activation(
-                    out=st[:, j, :], in_=T[("p1b", t, i, j)][:], func=ACT.Identity,
-                    bias=bias[t][:, j : j + 1], scale=1.0,
+                    out=st[:, j, :].rearrange("p (s b r) -> p b s r", b=2, r=HALF),
+                    in_=T[("p1b", t, i, j)][:].rearrange("p (b s r) -> p b s r", b=2, r=HALF),
+                    func=ACT.Identity, bias=bias[t][:, j : j + 1], scale=1.0,
                 )
             T[("st", t, i)] = st
 
@@ -240,7 +241,7 @@ def tile_scoperecognizer_t_kernel(tc, q, k, Wq, bq, Wk, bk, out):
             if not ok(i):
                 return
             for c in chunks:
-                c0 = 4 * (KREG * (c // L) + PADK + c % L)
+                c0 = 4 * (PADK + c)
                 nc.vector.tensor_tensor(
                     out=gk[i % 2][:, c0 : c0 + 4 * P].rearrange("p (r j) -> p r j", j=4),
                     in0=T[("p1a", "k", i, c)][:].rearrange("p j r -> p r j"),
@@ -253,13 +254,10 @@ def tile_scoperecognizer_t_kernel(tc, q, k, Wq, bq, Wk, bk, out):
                 return
             go = work.tile([P, 4 * BLK], BF16, name="gout_q", tag="gout_q", align_bytes=64)
             st = T[("st", "q", i)]
-            dst = go[:].rearrange("p (s b r j) -> p b s r j", b=2, r=HALF, j=4)
-            for bb in range(2):
-                nc.gpsimd.tensor_scalar(
-                    out=dst[:, bb],
-                    in0=st[:, :, bb * L : (bb + 1) * L].rearrange("p j (s r) -> p s r j", r=HALF),
-                    scalar1=1.0, scalar2=0.0, op0=ALU.mult, op1=ALU.add,
-                )
+            nc.gpsimd.tensor_scalar(
+                out=go[:].rearrange("p (r j) -> p r j", j=4), in0=st[:].rearrange("p j r -> p r j"),
+                scalar1=1.0, scalar2=0.0, op0=ALU.mult, op1=ALU.add,
+            )
             T[("gout", "q", i)] = go
 
         def quant(gr, g0, cod, sca, c0, n):
@@ -279,9 +277,8 @@ def tile_scoperecognizer_t_kernel(tc, q, k, Wq, bq, Wk, bk, out):
         def q2k(i):
             if not ok(i):
                 return
-            for bb in range(2):
-                quant(gk[i % 2], KREG * bb, ck[i % 2], sk[i % 2], KREG * bb, L)
-                quant(gk[i % 2], KREG * bb + L, ck[i % 2], sk[i % 2], KREG * bb + L, 32)
+            quant(gk[i % 2], 0, ck[i % 2], sk[i % 2], 0, BLK)
+            quant(gk[i % 2], BLK, ck[i % 2], sk[i % 2], BLK, GKW - BLK)
 
         def m2(i):
             if not ok(i):
@@ -291,7 +288,7 @@ def tile_scoperecognizer_t_kernel(tc, q, k, Wq, bq, Wk, bk, out):
                 for bb in range(2):
                     mx(
                         ps[:, s, :], cq[i % 2], sq[i % 2], s * QSLOT + bb * HALF,
-                        ck[i % 2], sk[i % 2], KREG * bb + s * HALF, P, bb == 0, bb == 1,
+                        ck[i % 2], sk[i % 2], L * bb + s * HALF, P, bb == 0, bb == 1,
                     )
             T[("p2", i)] = ps
 

@@ -358,7 +358,13 @@ def tile_scoperecognizer_t_kernel(tc, q, k, Wq, bq, Wk, bk, out):
 
         transposes("q", 0)
         w_transposes("q")
-        for c in range(-1, NB + 3):
+        def finish(i):
+            recip(i)
+            norm(i, (0, 1), "V")
+            norm(i, (2, 3), "S")
+            store(i)
+
+        for c in range(-1, NB + 1):
             first = c == -1
             tev("q", c + 1, "SV" if first else "SS")
             if first:
@@ -367,7 +373,7 @@ def tile_scoperecognizer_t_kernel(tc, q, k, Wq, bq, Wk, bk, out):
             if first:
                 w_transposes("k")
             s1("q", c)
-            recip(c - 3)
+            recip(c - 4)
             q1("k", c)
             if c == 0:
                 w_quantise("k")
@@ -380,17 +386,24 @@ def tile_scoperecognizer_t_kernel(tc, q, k, Wq, bq, Wk, bk, out):
                 w_quantise("q")
             if c == 0:
                 finish_mask()
-            norm(c - 3, (0, 1), "V")
+            norm(c - 4, (0, 1), "V")
             regroup(c)
             madd(c - 2)
             tev("k", c + 1, "SV" if first else "SS")
             if first:
                 w_evac("k", "VS")
-            norm(c - 3, (2, 3), "S")
-            store(c - 3)
+            norm(c - 4, (2, 3), "S")
+            store(c - 4)
             a_evac(c, (0,))
             rmax(c - 2)
             a_evac(c, (P, 2 * P, 3 * P))
             transposes("q", c + 2)
             m1b("q", c + 1)
-            ex(c - 2)
+            ex(c - 3)
+        ex(NB - 2)
+        finish(NB - 3)
+        madd(NB - 1)
+        rmax(NB - 1)
+        ex(NB - 1)
+        finish(NB - 2)
+        finish(NB - 1)

from contextlib import ExitStack

import concourse.mybir as mybir
from concourse.masks import make_identity

F32 = mybir.dt.float32
BF16 = mybir.dt.bfloat16
I32 = mybir.dt.int32
U32 = mybir.dt.uint32
U8 = mybir.dt.uint8
FP8X4 = mybir.dt.float8_e4m3fn_x4
ALU = mybir.AluOpType
ACT = mybir.ActivationFunctionType

P = 128
B, L, H = 32, 256, 512
BLK = 512
NB = B * L // BLK
HALF = 64
NS = L // HALF
PADK = 8
WIN = HALF + 2 * PADK
GKW = 544
CKW = 576
QSLOT = 192
NEG = -1.0e30
RAW_BUFS = 4
NOUT = 3

FLOPS = 2 * 2 * B * L * H * H + 2 * B * L * L * H


def tile_scoperecognizer_t_kernel(tc, q, k, Wq, bq, Wk, bk, out):
    nc = tc.nc
    src = {"q": q, "k": k}
    wsrc = {"q": Wq, "k": Wk}
    bsrc = {"q": bq, "k": bk}
    T = {}
    with ExitStack() as ctx:
        const = ctx.enter_context(tc.tile_pool(name="const", bufs=1))
        rawp = ctx.enter_context(tc.tile_pool(name="rawp", bufs=RAW_BUFS))
        work = ctx.enter_context(tc.tile_pool(name="work", bufs=2))
        pt = ctx.enter_context(tc.psum_pool(name="pt", bufs=2))
        p1 = ctx.enter_context(tc.psum_pool(name="p1", bufs=4))
        p2 = ctx.enter_context(tc.psum_pool(name="p2", bufs=2))
        ctx.enter_context(tc.manual_schedule())

        def ok(i):
            return 0 <= i < NB

        def load(t, i):
            if not ok(i):
                return
            r = rawp.tile([P, 4 * BLK], BF16, name="raw_" + t, tag="raw_" + t)
            nc.sync.dma_start(
                out=r[:].rearrange("p (b x) -> p b x", b=2),
                in_=src[t][2 * i : 2 * i + 2].rearrange("b (p s) c -> p b (s c)", s=2),
            )
            T[("raw", t, i)] = r

        wraw = {}
        braw = {}
        for t in ("q", "k"):
            braw[t] = const.tile([P, 4], BF16, name="braw_" + t)
            nc.scalar.dma_start(out=braw[t][:], in_=bsrc[t].rearrange("(m j) -> m j", j=4))
        for t in ("q", "k"):
            load(t, 0)
            wraw[t] = const.tile([P, 4 * H], BF16, name="wraw_" + t)
            nc.sync.dma_start(out=wraw[t][:], in_=wsrc[t].rearrange("(m j) c -> m (j c)", j=4))
        for i in range(1, RAW_BUFS):
            load("q", i)
            load("k", i)

        ident = const.tile([P, P], F32, name="ident")
        make_identity(nc, ident[:])
        warm = const.tile([P, 1], F32, name="warm")
        warm2 = const.tile([P, 1], F32, name="warm2")
        nc.vector.memset(warm[:], 0.0)
        nc.scalar.activation(out=warm2[:], in_=warm[:], func=ACT.Exp)

        cq, sq, ck, sk, gk = [], [], [], [], []
        for n in range(2):
            cq.append(const.tile([P, NS * QSLOT], U32, name="cq%d" % n, align_bytes=64))
            sq.append(const.tile([P, NS * QSLOT], U8, name="sq%d" % n, align_bytes=64))
            ck.append(const.tile([P, CKW], U32, name="ck%d" % n, align_bytes=64))
            sk.append(const.tile([P, CKW], U8, name="sk%d" % n, align_bytes=64))
            gk.append(const.tile([P, 4 * GKW], BF16, name="gk%d" % n, align_bytes=64))
            for x in (cq[n], sq[n], ck[n], sk[n]):
                nc.vector.memset(x[:].bitcast(I32), 0)
            nc.vector.memset(gk[n][:, 0 : 4 * PADK], 0.0)
            nc.vector.memset(gk[n][:, 4 * (PADK + BLK) : 4 * GKW], 0.0)

        m_lo = const.tile([P, WIN], F32, name="m_lo")
        m_hi = const.tile([P, WIN], F32, name="m_hi")
        for m_, off, side in ((m_lo, 0, -1), (m_hi, HALF, 1)):
            nc.gpsimd.memset(m_[:], 0.0)
            nc.gpsimd.affine_select(
                out=m_[:], in_=m_[:], compare_op=ALU.is_ge, fill=NEG,
                base=4 - PADK + off, pattern=[[1, WIN]], channel_multiplier=-1,
            )
            nc.gpsimd.affine_select(
                out=m_[:], in_=m_[:], compare_op=ALU.is_ge, fill=NEG,
                base=4 + PADK - off, pattern=[[-1, WIN]], channel_multiplier=1,
            )
            nc.gpsimd.affine_select(
                out=m_[:], in_=m_[:], compare_op=ALU.is_ge, fill=NEG,
                base=(HALF - 1) if side < 0 else -HALF, pattern=[[0, WIN]], channel_multiplier=side,
            )
        m_one = const.tile([P, WIN], F32, name="m_one")
        mask = const.tile([P, NS, WIN], F32, name="mask")

        def finish_mask():
            nc.vector.tensor_tensor(out=m_one[:], in0=m_lo[:], in1=m_hi[:], op=ALU.max)
            nc.vector.tensor_copy(out=mask[:], in_=m_one[:].unsqueeze(1).to_broadcast([P, NS, WIN]))
            nc.gpsimd.affine_select(
                out=mask[:, 0, :], in_=mask[:, 0, :], compare_op=ALU.is_ge, fill=NEG,
                base=-PADK, pattern=[[1, WIN]], channel_multiplier=0,
            )
            nc.gpsimd.affine_select(
                out=mask[:, NS - 1, :], in_=mask[:, NS - 1, :], compare_op=ALU.is_ge, fill=NEG,
                base=WIN - PADK - 1, pattern=[[-1, WIN]], channel_multiplier=0,
            )

        outs = []
        for n in range(NOUT):
            o = const.tile([P, NS, L], F32, name="o%d" % n)
            nc.gpsimd.memset(o[:], 0.0)
            outs.append(o)
        bias = {}
        for t in ("q", "k"):
            bias[t] = const.tile([P, 4], F32, name="bias_" + t)
            nc.vector.tensor_copy(out=bias[t][:], in_=braw[t][:])

        def copy_out(eng, dst, s_):
            if eng == "S":
                nc.scalar.copy(out=dst, in_=s_)
            else:
                nc.vector.tensor_copy(out=dst, in_=s_)

        W = {}

        def w_transposes(t):
            wf = wraw[t][:].bitcast(F32)
            for jj in range(2):
                ps = p1.tile([P, 4, P], F32, name="p1w", tag="p1")
                for g in range(4):
                    c = (4 * jj + g) * P
                    nc.tensor.transpose(out=ps[:, g, :], in_=wf[:, c : c + P], identity=ident[:])
                T[("pw", t, jj)] = ps

        def w_evac(t, engs):
            gw = const.tile([P, 4 * H], BF16, name="gw_" + t, align_bytes=64)
            gf = gw[:].bitcast(F32)
            for jj in range(2):
                copy_out(
                    engs[jj],
                    gf[:, jj * 512 : (jj + 1) * 512].rearrange("p (a m u) -> p a m u", a=2, u=2),
                    T[("pw", t, jj)][:].rearrange("p (a u) m -> p a m u", a=2),
                )
            T[("gw", t)] = gw

        def w_quantise(t):
            cw = const.tile([P, H], U32, name="cw_" + t, align_bytes=64)
            sw = const.tile([P, H], U8, name="sw_" + t, align_bytes=64)
            nc.vector.quantize_mx(out=cw[:].bitcast(FP8X4), scales=sw[:], in_=T[("gw", t)][:])
            W[t] = (cw, sw)

        def transposes(t, i):
            if not ok(i):
                return
            rf = T[("raw", t, i)][:].bitcast(F32)
            for bb in range(2):
                ps = pt.tile([P, 4, P], F32, name="pT", tag="pT")
                for g in range(4):
                    c = (4 * bb + g) * P
                    nc.tensor.transpose(out=ps[:, g, :], in_=rf[:, c : c + P], identity=ident[:])
                T[("pT", t, i, bb)] = ps
            load(t, i + RAW_BUFS)

        def tev(t, i, engs):
            if not ok(i):
                return
            g_ = work.tile([P, 4 * BLK], BF16, name="gin_" + t, tag="gin_" + t, align_bytes=64)
            gf = g_[:].bitcast(F32)
            for bb in range(2):
                copy_out(
                    engs[bb],
                    gf[:, bb * 512 : (bb + 1) * 512].rearrange("p (r g) -> p r g", g=4),
                    T[("pT", t, i, bb)][:].rearrange("p g r -> p r g"),
                )
            T[("gin", t, i)] = g_

        def q1(t, i):
            if not ok(i):
                return
            cod = work.tile([P, BLK], U32, name="cin" + t, tag="cin" + t, align_bytes=64)
            sca = work.tile([P, BLK], U8, name="sin" + t, tag="sin" + t, align_bytes=64)
            nc.vector.quantize_mx(out=cod[:].bitcast(FP8X4), scales=sca[:], in_=T[("gin", t, i)][:])
            T[("cin", t, i)] = (cod, sca)

        def mx(o, lc, ls, l0, rc, rs, r0, n, start, stop):
            nc.tensor.matmul_mx(
                out=o,
                lhsT=lc[:, l0 : l0 + P].bitcast(FP8X4), lhsT_scale=ls[:, l0 : l0 + P],
                rhs=rc[:, r0 : r0 + n].bitcast(FP8X4), rhs_scale=rs[:, r0 : r0 + n],
                start=start, stop=stop,
            )

        def m1b(t, i):
            if not ok(i):
                return
            cod, sca = T[("cin", t, i)]
            for j in range(4):
                ps = p1.tile([P, BLK], F32, name="p1b", tag="p1")
                mx(ps[:], W[t][0], W[t][1], j * P, cod, sca, 0, BLK, True, True)
                T[("p1b", t, i, j)] = ps

        def m1a(t, i):
            if not ok(i):
                return
            cod, sca = T[("cin", t, i)]
            for c in range(0, BLK, P):
                ps = p1.tile([P, 4, P], F32, name="p1a", tag="p1")
                for j in range(4):
                    mx(ps[:, j, :], W[t][0], W[t][1], j * P, cod, sca, c, P, True, True)
                T[("p1a", t, i, c)] = ps

        def s1(t, i):
            if not ok(i):
                return
            st = work.tile([P, 4, BLK], BF16, name="st_" + t, tag="st_" + t)
            for j in range(4):
                nc.scalar.activation(
                    out=st[:, j, :].rearrange("p (s b r) -> p b s r", b=2, r=HALF),
                    in_=T[("p1b", t, i, j)][:].rearrange("p (b s r) -> p b s r", b=2, r=HALF),
                    func=ACT.Identity, bias=bias[t][:, j : j + 1], scale=1.0,
                )
            T[("st", t, i)] = st

        def a_evac(i, chunks):
            if not ok(i):
                return
            for c in chunks:
                c0 = 4 * (PADK + c)
                nc.vector.tensor_tensor(
                    out=gk[i % 2][:, c0 : c0 + 4 * P].rearrange("p (r j) -> p r j", j=4),
                    in0=T[("p1a", "k", i, c)][:].rearrange("p j r -> p r j"),
                    in1=bias["k"][:].unsqueeze(1).to_broadcast([P, P, 4]),
                    op=ALU.add,
                )

        def regroup(i):
            if not ok(i):
                return
            go = work.tile([P, 4 * BLK], BF16, name="gout_q", tag="gout_q", align_bytes=64)
            st = T[("st", "q", i)]
            nc.gpsimd.tensor_scalar(
                out=go[:].rearrange("p (r j) -> p r j", j=4), in0=st[:].rearrange("p j r -> p r j"),
                scalar1=1.0, scalar2=0.0, op0=ALU.mult, op1=ALU.add,
            )
            T[("gout", "q", i)] = go

        def quant(gr, g0, cod, sca, c0, n):
            nc.vector.quantize_mx(
                out=cod[:, c0 : c0 + n].bitcast(FP8X4), scales=sca[:, c0 : c0 + n], in_=gr[:, 4 * g0 : 4 * (g0 + n)]
            )

        def q2q(i):
            if not ok(i):
                return
            go = T[("gout", "q", i)]
            quant(go, 0, cq[i % 2], sq[i % 2], 0, HALF)
            for s in range(NS - 1):
                quant(go, (2 * s + 1) * HALF, cq[i % 2], sq[i % 2], s * QSLOT + P, P)
            quant(go, (2 * NS - 1) * HALF, cq[i % 2], sq[i % 2], (NS - 1) * QSLOT + P, HALF)

        def q2k(i):
            if not ok(i):
                return
            quant(gk[i % 2], 0, ck[i % 2], sk[i % 2], 0, BLK)
            quant(gk[i % 2], BLK, ck[i % 2], sk[i % 2], BLK, GKW - BLK)

        def m2(i):
            if not ok(i):
                return
            ps = p2.tile([P, NS, P], F32, name="p2t", tag="p2")
            for s in range(NS):
                for bb in range(2):
                    mx(
                        ps[:, s, :], cq[i % 2], sq[i % 2], s * QSLOT + bb * HALF,
                        ck[i % 2], sk[i % 2], L * bb + s * HALF, P, bb == 0, bb == 1,
                    )
            T[("p2", i)] = ps

        def madd(i):
            if not ok(i):
                return
            y = work.tile([P, NS, WIN], F32, name="y", tag="y")
            nc.vector.tensor_tensor(out=y[:], in0=T[("p2", i)][:, :, 0:WIN], in1=mask[:], op=ALU.add)
            T[("y", i)] = y

        def rmax(i):
            if not ok(i):
                return
            nm = work.tile([P, NS], F32, name="nm", tag="nm")
            nc.vector.tensor_reduce(
                out=nm[:], in_=T[("y", i)][:], axis=mybir.AxisListType.X, op=ALU.max, negate=True
            )
            T[("nm", i)] = nm

        def span(s):
            return (PADK if s == 0 else 0), (WIN - PADK if s == NS - 1 else WIN)

        def window(i, s):
            n0, n1 = span(s)
            return outs[i % NOUT][:, s, s * HALF - PADK + n0 : s * HALF - PADK + n1]

        def ex(i):
            if not ok(i):
                return
            y = T[("y", i)]
            nm = T[("nm", i)]
            sm = work.tile([P, NS], F32, name="sm", tag="sm")
            for s in range(NS):
                n0, n1 = span(s)
                nc.scalar.activation(
                    out=window(i, s), in_=y[:, s, n0:n1], func=ACT.Exp,
                    bias=nm[:, s : s + 1], scale=1.0, accum_out=sm[:, s : s + 1],
                )
            T[("sm", i)] = sm

        def recip(i):
            if not ok(i):
                return
            rc = work.tile([P, NS], F32, name="rc", tag="rc")
            nc.vector.reciprocal(out=rc[:], in_=T[("sm", i)][:])
            T[("rc", i)] = rc

        def norm(i, tiles, eng):
            if not ok(i):
                return
            rc = T[("rc", i)]
            for s in tiles:
                w = window(i, s)
                if eng == "V":
                    nc.vector.tensor_scalar_mul(out=w, in0=w, scalar1=rc[:, s : s + 1])
                else:
                    nc.scalar.activation(out=w, in_=w, func=ACT.Copy, scale=rc[:, s : s + 1])

        def store(i):
            if not ok(i):
                return
            for bb in range(2):
                nc.sync.dma_start(
                    out=out[2 * i + bb].rearrange("(s p) j -> p s j", p=HALF),
                    in_=outs[i % NOUT][bb * HALF : (bb + 1) * HALF, :, :],
                )

        transposes("q", 0)
        w_transposes("q")
        def finish(i):
            recip(i)
            norm(i, (0, 1), "V")
            norm(i, (2, 3), "S")
            store(i)

        for c in range(-1, NB + 1):
            first = c == -1
            tev("q", c + 1, "SV" if first else "SS")
            if first:
                w_evac("q", "VS")
            transposes("k", c + 1)
            if first:
                w_transposes("k")
            s1("q", c)
            recip(c - 4)
            q1("k", c)
            if c == 0:
                w_quantise("k")
            m1a("k", c)
            q2q(c - 1)
            q2k(c - 1)
            m2(c - 1)
            q1("q", c + 1)
            if first:
                w_quantise("q")
            if c == 0:
                finish_mask()
            norm(c - 4, (0, 1), "V")
            regroup(c)
            madd(c - 2)
            tev("k", c + 1, "SV" if first else "SS")
            if first:
                w_evac("k", "VS")
            norm(c - 4, (2, 3), "S")
            store(c - 4)
            a_evac(c, (0,))
            rmax(c - 2)
            a_evac(c, (P, 2 * P, 3 * P))
            transposes("q", c + 2)
            m1b("q", c + 1)
            ex(c - 3)
        ex(NB - 2)
        finish(NB - 3)
        madd(NB - 1)
        rmax(NB - 1)
        ex(NB - 1)
        finish(NB - 2)
        finish(NB - 1)
